import numpy as np
import ml_dtypes


def mxq(x, axis, fmt="e4m3"):
    dtype, down = {"e4m3": (ml_dtypes.float8_e4m3fn, 7), "e5m2": (ml_dtypes.float8_e5m2, 14)}[fmt]
    v = np.moveaxis(np.asarray(x, np.float32).astype(ml_dtypes.bfloat16).astype(np.float64), axis, -1)
    blocks = v.reshape(v.shape[:-1] + (-1, 32))
    amax = np.abs(blocks).max(-1, keepdims=True)
    byte = np.maximum(np.where(amax > 0, np.frexp(amax)[1] - 1 + 127, 0) - down, 1)
    scale = np.exp2(byte - 127.0)
    codes = (blocks / scale).astype(np.float32).astype(dtype).astype(np.float64)
    return np.moveaxis((codes * scale).reshape(v.shape), -1, axis)


WIDE = False


def mx_kscale(k):
    if not WIDE:
        return np.ones(k)
    levels = np.array([10, -10, 5, -5, 0])
    if k % 512:
        return np.exp2(np.random.permutation(np.resize(levels, k // 32))).repeat(32)
    a = np.empty((k // 512, 16))
    for p in range(k // 512):
        a[p, :8] = np.random.permutation(np.resize(levels, 8))
        for g in range(8):
            far = levels[np.abs(levels - a[p, g]) >= 10]
            a[p, g + 8] = far[np.random.randint(len(far))]
    return np.exp2(a.ravel()).repeat(32)


BF16 = ml_dtypes.bfloat16


def bf(x):
    return np.asarray(x, np.float32).astype(BF16)


def f64(x):
    return np.asarray(x).astype(np.float64)


B, IN, NLVL, KLVL, C, CM, CO, OU, OV = 64, 256, 4, 1, 256, 1024, 256, 8, 8
NK = 2 ** KLVL
S = 2 ** (NLVL - KLVL)
KA, KB = 4 * C, 4 * CM


def patches(x):
    U, V, Bn, H, W, Cc = x.shape
    return x.reshape(U, V, Bn, H // 2, 2, W // 2, 2, Cc).swapaxes(4, 5).reshape(U, V, Bn * (H // 2) * (W // 2), 4 * Cc)


def node_conv(x, w, b):
    U, V, Bn, H, W, Cc = x.shape
    Co = w.shape[-1]
    y = (mxq(patches(x), 3, "e4m3") @ mxq(w.reshape(U, V, 4 * Cc, Co), 2, "e4m3")) + b[:, :, None, :]
    return np.maximum(y, 0.0).reshape(U, V, Bn, H // 2, W // 2, Co)


def setup_inputs():
    s = mx_kscale(KA).reshape(2, 2, C)
    t = mx_kscale(KB)[:CM]
    x = np.maximum(np.random.standard_normal((NK, NK, B, S, S, C)), 0.0) * np.tile(s, (S // 2, S // 2, 1))
    return {"x_leaf": bf(x),
            "f_first": bf(np.random.standard_normal((NK, NK, 2, 2, C, CM)) * np.sqrt(0.5 / C) / s[:, :, :, None] * t),
            "b_first": bf(np.random.standard_normal((NK, NK, CM)) * 0.2 * t),
            "f_second": bf(np.random.standard_normal((NK, NK, 2, 2, CM, CO)) * np.sqrt(0.5 / CM) / t[:, None]),
            "b_second": bf(np.random.standard_normal((NK, NK, CO)) * 0.2)}


def reference(x_leaf, f_first, b_first, f_second, b_second):
    h = node_conv(f64(x_leaf), f64(f_first), f64(b_first))
    return node_conv(h, f64(f_second), f64(b_second))

@@ -1,0 +1,301 @@
+from contextlib import ExitStack
+
+import concourse.mybir as mybir
+from concourse.masks import make_identity
+
+BF16 = mybir.dt.bfloat16
+F32 = mybir.dt.float32
+U32 = mybir.dt.uint32
+U8 = mybir.dt.uint8
+FP8X4 = mybir.dt.float8_e4m3fn_x4
+RELU = mybir.ActivationFunctionType.Relu
+ADD = mybir.AluOpType.add
+
+P = 128
+PACK = 4
+HALVES = 8
+HALF_SAMPLES = 32
+C_MID = 1024
+C_OUT = 256
+CHUNKS = C_MID // P
+COLS = 512
+RAW = 4096
+QUARTER = 512
+SET_WORDS = 4 * QUARTER
+LOADS_AHEAD = 3
+SHARED_QUARTER = 1
+SCALAR_GROUPS = 96
+
+FLOPS = 2 * 4 * (1024 * 1024 * 1024 + 256 * 4096 * 256)
+
+
+def tile_butterflylayer2d_pb_t_kernel(tc, x_leaf, f_first, b_first, f_second, b_second, out):
+    nc = tc.nc
+    with ExitStack() as ctx:
+        consts = ctx.enter_context(tc.tile_pool(name="consts", bufs=1))
+        raw_pool = ctx.enter_context(tc.tile_pool(name="raw", bufs=3 * LOADS_AHEAD))
+        grouped_pool = ctx.enter_context(tc.tile_pool(name="grouped", bufs=4))
+        set_pool = ctx.enter_context(tc.tile_pool(name="sets", bufs=3))
+        code_pool = ctx.enter_context(tc.tile_pool(name="codes", bufs=2))
+        out_pool = ctx.enter_context(tc.tile_pool(name="outs", bufs=2))
+        psum_x = ctx.enter_context(tc.psum_pool(name="psum_x", bufs=2))
+        psum_h = ctx.enter_context(tc.psum_pool(name="psum_h", bufs=5))
+        psum_out = ctx.enter_context(tc.psum_pool(name="psum_out", bufs=1))
+
+        identity = consts.tile([P, P], F32)
+        make_identity(nc, identity[:])
+
+        bias_first = consts.tile([P, 4 * CHUNKS], BF16)
+        with nc.allow_non_contiguous_dma(reason="a 8 KiB bias in runs of 4 values"):
+            nc.scalar.dma_start(
+                out=bias_first[:].rearrange("w (n lo) -> w n lo", lo=4),
+                in_=b_first.rearrange("i j (hi w lo) -> w (i j hi) lo", hi=2, lo=4),
+            )
+        ones = consts.tile([P, P], BF16)
+        nc.vector.memset(ones[:], 1.0)
+        bias_row = consts.tile([P, 4 * C_OUT], BF16)
+        nc.vector.memset(bias_row[:], 0.0)
+        nc.scalar.dma_start(out=bias_row[0:1, :], in_=b_second.rearrange("(one i) j c -> one (i j c)", one=1))
+
+        x_raw = {}
+        w_raw = {}
+        x_grouped = {}
+        w_grouped = {}
+        h_raw = {}
+        h_grouped = {}
+        x_mx = {}
+        w_mx = {}
+        h_mx = {}
+        bias_second = {}
+        acc_out = {}
+        summed = {}
+
+        def load(half):
+            i, j = divmod(half // 2, 2)
+            first = (half % 2) * HALF_SAMPLES
+            pixels = raw_pool.tile([P, RAW], BF16, tag="raw")
+            nc.sync.dma_start(
+                out=pixels[:],
+                in_=x_leaf[i, j, first : first + HALF_SAMPLES].rearrange("n (yh p) x c -> (n yh) (p x c)", p=2),
+            )
+            x_raw[half] = pixels
+            for piece in range(2):
+                rows = raw_pool.tile([P, RAW], BF16, tag="raw")
+                if half % 2 == 0:
+                    nc.sync.dma_start(
+                        out=rows[:],
+                        in_=f_first[i, j, piece].rearrange("q (c t) o -> (q c) (t o)", t=PACK),
+                    )
+                else:
+                    nc.sync.dma_start(
+                        out=rows[:].rearrange("w (g r) -> w g r", g=4),
+                        in_=f_second[i, j, piece].rearrange("q (hi w t) o -> w (q hi) (t o)", hi=2, t=PACK),
+                    )
+                w_raw[(half, piece)] = rows
+
+        def transpose_x(half):
+            words = x_raw[half][:].bitcast(F32)
+            for p in range(2):
+                grouped = grouped_pool.tile([P, PACK * COLS], BF16, tag="x_grouped", align_bytes=64)
+                x_grouped[(half, p)] = grouped
+                for q2 in range(2):
+                    bank = psum_x.tile([P, 4, P], F32, tag="x_bank")
+                    for a in range(4):
+                        x2, u = divmod(a, 2)
+                        first = (8 * p + 2 * (2 * x2 + q2)) * P
+                        nc.tensor.transpose(bank[:, a, :], words[:, first + u : first + 2 * P : 2], identity[:])
+                    nc.scalar.copy(
+                        out=grouped[:]
+                        .bitcast(F32)
+                        .rearrange("w (p2 q2 s a) -> w q2 p2 s a", p2=2, q2=2, a=4)[:, q2],
+                        in_=bank[:].rearrange("w a (s p2) -> w p2 s a", p2=2),
+                    )
+
+        def quantise_x(half, p):
+            if p == 0:
+                codes = code_pool.tile([P, 2 * COLS], U32, tag="x_codes", align_bytes=64)
+                scales = code_pool.tile([P, 2 * COLS], U8, tag="x_scales", align_bytes=64)
+                x_mx[half] = (codes, scales)
+            codes, scales = x_mx[half]
+            cols = slice(p * COLS, (p + 1) * COLS)
+            nc.vector.quantize_mx(
+                out=codes[:, cols].bitcast(FP8X4), scales=scales[:, cols], in_=x_grouped[(half, p)][:]
+            )
+
+        def regroup_w(w_set, quarter):
+            grouped = grouped_pool.tile([P, PACK * QUARTER], BF16, tag="w_grouped", align_bytes=64)
+            w_grouped[quarter] = grouped
+            rows = w_raw[(w_set, quarter // 2)]
+            if w_set % 2 == 0:
+                source = rows[:].rearrange("w (t h c i) -> w h c t i", t=PACK, h=2, i=4)[:, quarter % 2]
+                columns = grouped[:].rearrange("w (i c t) -> w c t i", i=4, t=PACK)
+                if quarter == SHARED_QUARTER:
+                    nc.scalar.copy(out=columns[:, :SCALAR_GROUPS], in_=source[:, :SCALAR_GROUPS])
+                    nc.vector.tensor_copy(out=columns[:, SCALAR_GROUPS:], in_=source[:, SCALAR_GROUPS:])
+                else:
+                    nc.vector.tensor_copy(out=columns, in_=source)
+            else:
+                source = rows[:].rearrange("w (h g t c i) -> w h g c t i", h=2, g=2, t=PACK, i=4)[:, quarter % 2]
+                columns = grouped[:].rearrange("w (g c i t) -> w g c t i", g=2, i=4, t=PACK)
+                if quarter == SHARED_QUARTER:
+                    rest = SCALAR_GROUPS - 64
+                    nc.scalar.copy(out=columns[:, 0], in_=source[:, 0])
+                    nc.scalar.copy(out=columns[:, 1, :rest], in_=source[:, 1, :rest])
+                    nc.vector.tensor_copy(out=columns[:, 1, rest:], in_=source[:, 1, rest:])
+                else:
+                    nc.vector.tensor_copy(out=columns, in_=source)
+
+        def quantise_w(w_set, quarter):
+            if quarter == 0:
+                codes = set_pool.tile([P, SET_WORDS], U32, tag="w_codes", align_bytes=64)
+                scales = set_pool.tile([P, SET_WORDS], U8, tag="w_scales", align_bytes=64)
+                w_mx[w_set] = (codes, scales)
+            codes, scales = w_mx[w_set]
+            cols = slice(quarter * QUARTER, (quarter + 1) * QUARTER)
+            nc.vector.quantize_mx(
+                out=codes[:, cols].bitcast(FP8X4), scales=scales[:, cols], in_=w_grouped[quarter][:]
+            )
+
+        def first_conv(half, chunk):
+            node = half // 2
+            w_codes, w_scales = w_mx[2 * node]
+            x_codes, x_scales = x_mx[half]
+            acc = psum_h.tile([P, COLS], F32, tag="acc_h")
+            for p in range(2):
+                w_cols = slice(p * C_MID + chunk * P, p * C_MID + (chunk + 1) * P)
+                x_cols = slice(p * COLS, (p + 1) * COLS)
+                nc.tensor.matmul_mx(
+                    out=acc[:],
+                    lhsT=w_codes[:, w_cols].bitcast(FP8X4),
+                    lhsT_scale=w_scales[:, w_cols],
+                    rhs=x_codes[:, x_cols].bitcast(FP8X4),
+                    rhs_scale=x_scales[:, x_cols],
+                    start=(p == 0),
+                    stop=(p == 1),
+                )
+            if chunk % 4 == 0:
+                h_raw[(half, chunk // 4)] = grouped_pool.tile(
+                    [P, 4 * COLS], BF16, tag="h_raw", name="h_raw", align_bytes=64
+                )
+            nc.scalar.activation(
+                out=h_raw[(half, chunk // 4)][:, chunk % 4 * COLS : (chunk % 4 + 1) * COLS],
+                in_=acc[:],
+                func=RELU,
+                bias=bias_first[:, node * CHUNKS + chunk : node * CHUNKS + chunk + 1],
+                scale=1.0,
+            )
+
+        def regroup_h(half, group):
+            grouped = grouped_pool.tile([P, PACK * COLS], BF16, tag="h_grouped", align_bytes=64)
+            h_grouped[(half, group)] = grouped
+            nc.vector.tensor_copy(
+                out=grouped[:].rearrange("w (c i t) -> w c t i", i=4, t=PACK),
+                in_=h_raw[(half, group)][:].rearrange("w (t c i) -> w c t i", t=PACK, i=4),
+            )
+
+        def quantise_h(half, group):
+            if group == 0:
+                codes = code_pool.tile([P, CHUNKS * P], U32, tag="h_codes", align_bytes=64)
+                scales = code_pool.tile([P, CHUNKS * P], U8, tag="h_scales", align_bytes=64)
+                h_mx[half] = (codes, scales)
+            codes, scales = h_mx[half]
+            cols = slice(group * 4 * P, (group + 1) * 4 * P)
+            nc.vector.quantize_mx(
+                out=codes[:, cols].bitcast(FP8X4),
+                scales=scales[:, cols],
+                in_=h_grouped[(half, group)][:],
+            )
+
+        def spread_bias(node):
+            spread = psum_h.tile([P, COLS], F32, tag="acc_h")
+            nc.tensor.matmul(
+                out=spread[:, :C_OUT],
+                lhsT=ones[:],
+                rhs=bias_row[:, node * C_OUT : (node + 1) * C_OUT],
+                start=True,
+                stop=True,
+            )
+            bias_second[node] = out_pool.tile([P, C_OUT], F32, tag="bias_second", name="bias_second")
+            nc.scalar.copy(out=bias_second[node][:], in_=spread[:, :C_OUT])
+
+        def second_conv(half):
+            h_codes, h_scales = h_mx[half]
+            w_codes, w_scales = w_mx[2 * (half // 2) + 1]
+            acc = psum_out.tile([P, C_OUT], F32, tag="acc_out")
+            acc_out[half] = acc
+            for chunk in range(CHUNKS):
+                hi, place = divmod(chunk, 4)
+                h_cols = slice(chunk * P, (chunk + 1) * P)
+                w_cols = slice((2 * place + hi) * C_OUT, (2 * place + hi + 1) * C_OUT)
+                nc.tensor.matmul_mx(
+                    out=acc[:],
+                    lhsT=h_codes[:, h_cols].bitcast(FP8X4),
+                    lhsT_scale=h_scales[:, h_cols],
+                    rhs=w_codes[:, w_cols].bitcast(FP8X4),
+                    rhs_scale=w_scales[:, w_cols],
+                    start=(chunk == 0),
+                    stop=(chunk == CHUNKS - 1),
+                )
+
+        def add_bias(half):
+            node = half // 2
+            summed[half] = out_pool.tile([P, C_OUT], F32, tag="summed", name="summed")
+            nc.vector.tensor_tensor(
+                out=summed[half][:],
+                in0=acc_out[half][:],
+                in1=bias_second[node][:],
+                op=ADD,
+            )
+
+        def relu_and_store(half):
+            i, j = divmod(half // 2, 2)
+            first = (half % 2) * HALF_SAMPLES
+            result = out_pool.tile([P, C_OUT], F32, tag="result")
+            nc.scalar.activation(out=result[:], in_=summed[half][:], func=RELU)
+            nc.scalar.dma_start(
+                out=out[i, j, first : first + HALF_SAMPLES].rearrange("n y x c -> (n y x) c"), in_=result[:]
+            )
+
+        for half in range(LOADS_AHEAD):
+            load(half)
+        for step in range(HALVES + 2):
+            preparing = step < HALVES
+            convolving = 1 <= step <= HALVES
+            finishing = step >= 2
+            if finishing:
+                regroup_h(step - 2, 1)
+            if preparing:
+                regroup_w(step, 1)
+                transpose_x(step)
+            if finishing:
+                quantise_h(step - 2, 1)
+                if step % 2 == 0:
+                    spread_bias((step - 2) // 2)
+                second_conv(step - 2)
+            if preparing:
+                regroup_w(step, 0)
+                regroup_w(step, 2)
+                quantise_w(step, 0)
+                quantise_x(step, 0)
+                quantise_w(step, 2)
+                quantise_x(step, 1)
+                quantise_w(step, 1)
+            if finishing:
+                add_bias(step - 2)
+            if convolving:
+                for chunk in range(4):
+                    first_conv(step - 1, chunk)
+            if finishing:
+                relu_and_store(step - 2)
+            if preparing:
+                regroup_w(step, 3)
+                if step + LOADS_AHEAD < HALVES:
+                    load(step + LOADS_AHEAD)
+            if convolving:
+                regroup_h(step - 1, 0)
+            if preparing:
+                quantise_w(step, 3)
+            if convolving:
+                quantise_h(step - 1, 0)
+                for chunk in range(4, CHUNKS):
+                    first_conv(step - 1, chunk)

@@ -23,8 +23,7 @@ RAW = 4096
 QUARTER = 512
 SET_WORDS = 4 * QUARTER
 LOADS_AHEAD = 3
-SHARED_QUARTER = 1
-SCALAR_GROUPS = 96
+SCALAR_PARTS = (0, 2, 0, 1)
 
 FLOPS = 2 * 4 * (1024 * 1024 * 1024 + 256 * 4096 * 256)
 
@@ -45,6 +44,10 @@ def tile_butterflylayer2d_pb_t_kernel(tc, x_leaf, f_first, b_first, f_second, b_
         identity = consts.tile([P, P], F32)
         make_identity(nc, identity[:])
 
+        warm = consts.tile([P, 1], F32)
+        nc.gpsimd.memset(warm[:], 0.0)
+        nc.scalar.activation(out=warm[:], in_=warm[:], func=RELU)
+
         bias_first = consts.tile([P, 4 * CHUNKS], BF16)
         with nc.allow_non_contiguous_dma(reason="a 8 KiB bias in runs of 4 values"):
             nc.scalar.dma_start(
@@ -52,9 +55,9 @@ def tile_butterflylayer2d_pb_t_kernel(tc, x_leaf, f_first, b_first, f_second, b_
                 in_=b_first.rearrange("i j (hi w lo) -> w (i j hi) lo", hi=2, lo=4),
             )
         ones = consts.tile([P, P], BF16)
-        nc.vector.memset(ones[:], 1.0)
+        nc.gpsimd.memset(ones[:], 1.0)
         bias_row = consts.tile([P, 4 * C_OUT], BF16)
-        nc.vector.memset(bias_row[:], 0.0)
+        nc.gpsimd.memset(bias_row[:], 0.0)
         nc.scalar.dma_start(out=bias_row[0:1, :], in_=b_second.rearrange("(one i) j c -> one (i j c)", one=1))
 
         x_raw = {}
@@ -70,46 +73,58 @@ def tile_butterflylayer2d_pb_t_kernel(tc, x_leaf, f_first, b_first, f_second, b_
         acc_out = {}
         summed = {}
 
-        def load(half):
+        def load_x(half, p):
             i, j = divmod(half // 2, 2)
             first = (half % 2) * HALF_SAMPLES
-            pixels = raw_pool.tile([P, RAW], BF16, tag="raw")
+            if p == 0:
+                x_raw[half] = raw_pool.tile([P, RAW], BF16, tag="raw", name="x_rows")
             nc.sync.dma_start(
-                out=pixels[:],
-                in_=x_leaf[i, j, first : first + HALF_SAMPLES].rearrange("n (yh p) x c -> (n yh) (p x c)", p=2),
+                out=x_raw[half][:, p * RAW // 2 : (p + 1) * RAW // 2],
+                in_=x_leaf[i, j, first : first + HALF_SAMPLES].rearrange("n (yh p) x c -> p (n yh) (x c)", p=2)[p],
             )
-            x_raw[half] = pixels
-            for piece in range(2):
-                rows = raw_pool.tile([P, RAW], BF16, tag="raw")
-                if half % 2 == 0:
-                    nc.sync.dma_start(
-                        out=rows[:],
-                        in_=f_first[i, j, piece].rearrange("q (c t) o -> (q c) (t o)", t=PACK),
-                    )
-                else:
-                    nc.sync.dma_start(
-                        out=rows[:].rearrange("w (g r) -> w g r", g=4),
-                        in_=f_second[i, j, piece].rearrange("q (hi w t) o -> w (q hi) (t o)", hi=2, t=PACK),
-                    )
-                w_raw[(half, piece)] = rows
 
-        def transpose_x(half):
+        def load_w(half, piece):
+            i, j = divmod(half // 2, 2)
+            rows = raw_pool.tile([P, RAW], BF16, tag="raw", name="w_rows")
+            w_raw[(half, piece)] = rows
+            if half == 0:
+                source = f_first[i, j, piece].rearrange("q (c t) (h o) -> h (q c) t o", t=PACK, h=2)
+                for hi in range(2):
+                    part = rows[:, hi * RAW // 2 : (hi + 1) * RAW // 2]
+                    nc.sync.dma_start(out=part.rearrange("w (t o) -> w t o", t=PACK), in_=source[hi])
+            elif half % 2 == 0:
+                nc.sync.dma_start(
+                    out=rows[:],
+                    in_=f_first[i, j, piece].rearrange("q (c t) o -> (q c) (t o)", t=PACK),
+                )
+            else:
+                nc.sync.dma_start(
+                    out=rows[:].rearrange("w (g r) -> w g r", g=4),
+                    in_=f_second[i, j, piece].rearrange("q (hi w t) o -> w (q hi) (t o)", hi=2, t=PACK),
+                )
+
+        def load(half):
+            load_w(half, 0)
+            load_x(half, 0)
+            load_x(half, 1)
+            load_w(half, 1)
+
+        def transpose_x(half, p):
             words = x_raw[half][:].bitcast(F32)
-            for p in range(2):
-                grouped = grouped_pool.tile([P, PACK * COLS], BF16, tag="x_grouped", align_bytes=64)
-                x_grouped[(half, p)] = grouped
-                for q2 in range(2):
-                    bank = psum_x.tile([P, 4, P], F32, tag="x_bank")
-                    for a in range(4):
-                        x2, u = divmod(a, 2)
-                        first = (8 * p + 2 * (2 * x2 + q2)) * P
-                        nc.tensor.transpose(bank[:, a, :], words[:, first + u : first + 2 * P : 2], identity[:])
-                    nc.scalar.copy(
-                        out=grouped[:]
-                        .bitcast(F32)
-                        .rearrange("w (p2 q2 s a) -> w q2 p2 s a", p2=2, q2=2, a=4)[:, q2],
-                        in_=bank[:].rearrange("w a (s p2) -> w p2 s a", p2=2),
-                    )
+            grouped = grouped_pool.tile([P, PACK * COLS], BF16, tag="x_grouped", align_bytes=64)
+            x_grouped[(half, p)] = grouped
+            for q2 in range(2):
+                bank = psum_x.tile([P, 4, P], F32, tag="x_bank")
+                for a in range(4):
+                    x2, u = divmod(a, 2)
+                    first = (8 * p + 2 * (2 * x2 + q2)) * P
+                    nc.tensor.transpose(bank[:, a, :], words[:, first + u : first + 2 * P : 2], identity[:])
+                nc.scalar.copy(
+                    out=grouped[:]
+                    .bitcast(F32)
+                    .rearrange("w (p2 q2 s a) -> w q2 p2 s a", p2=2, q2=2, a=4)[:, q2],
+                    in_=bank[:].rearrange("w a (s p2) -> w p2 s a", p2=2),
+                )
 
         def quantise_x(half, p):
             if p == 0:
@@ -122,28 +137,34 @@ def tile_butterflylayer2d_pb_t_kernel(tc, x_leaf, f_first, b_first, f_second, b_
                 out=codes[:, cols].bitcast(FP8X4), scales=scales[:, cols], in_=x_grouped[(half, p)][:]
             )
 
-        def regroup_w(w_set, quarter):
-            grouped = grouped_pool.tile([P, PACK * QUARTER], BF16, tag="w_grouped", align_bytes=64)
-            w_grouped[quarter] = grouped
+        def views_w(w_set, quarter):
+            if (w_set, quarter) not in w_grouped:
+                w_grouped[(w_set, quarter)] = grouped_pool.tile(
+                    [P, PACK * QUARTER], BF16, tag="w_grouped", name="w_grouped", align_bytes=64
+                )
+            grouped = w_grouped[(w_set, quarter)]
             rows = w_raw[(w_set, quarter // 2)]
             if w_set % 2 == 0:
-                source = rows[:].rearrange("w (t h c i) -> w h c t i", t=PACK, h=2, i=4)[:, quarter % 2]
-                columns = grouped[:].rearrange("w (i c t) -> w c t i", i=4, t=PACK)
-                if quarter == SHARED_QUARTER:
-                    nc.scalar.copy(out=columns[:, :SCALAR_GROUPS], in_=source[:, :SCALAR_GROUPS])
-                    nc.vector.tensor_copy(out=columns[:, SCALAR_GROUPS:], in_=source[:, SCALAR_GROUPS:])
-                else:
-                    nc.vector.tensor_copy(out=columns, in_=source)
+                order = "w (h t g c i) -> w h g c t i" if w_set == 0 else "w (t h g c i) -> w h g c t i"
+                source = rows[:].rearrange(order, t=PACK, h=2, g=2, i=4)[:, quarter % 2]
+                columns = grouped[:].rearrange("w (i g c t) -> w g c t i", i=4, g=2, t=PACK)
             else:
                 source = rows[:].rearrange("w (h g t c i) -> w h g c t i", h=2, g=2, t=PACK, i=4)[:, quarter % 2]
                 columns = grouped[:].rearrange("w (g c i t) -> w g c t i", g=2, i=4, t=PACK)
-                if quarter == SHARED_QUARTER:
-                    rest = SCALAR_GROUPS - 64
-                    nc.scalar.copy(out=columns[:, 0], in_=source[:, 0])
-                    nc.scalar.copy(out=columns[:, 1, :rest], in_=source[:, 1, :rest])
-                    nc.vector.tensor_copy(out=columns[:, 1, rest:], in_=source[:, 1, rest:])
-                else:
-                    nc.vector.tensor_copy(out=columns, in_=source)
+            return columns, source
+
+        def regroup_w_scalar(w_set, quarter):
+            columns, source = views_w(w_set, quarter)
+            for part in range(SCALAR_PARTS[quarter]):
+                nc.scalar.copy(out=columns[:, part], in_=source[:, part])
+
+        def regroup_w(w_set, quarter):
+            columns, source = views_w(w_set, quarter)
+            mine = SCALAR_PARTS[quarter]
+            if mine == 0:
+                nc.vector.tensor_copy(out=columns, in_=source)
+            elif mine == 1:
+                nc.vector.tensor_copy(out=columns[:, 1], in_=source[:, 1])
 
         def quantise_w(w_set, quarter):
             if quarter == 0:
@@ -153,7 +174,7 @@ def tile_butterflylayer2d_pb_t_kernel(tc, x_leaf, f_first, b_first, f_second, b_
             codes, scales = w_mx[w_set]
             cols = slice(quarter * QUARTER, (quarter + 1) * QUARTER)
             nc.vector.quantize_mx(
-                out=codes[:, cols].bitcast(FP8X4), scales=scales[:, cols], in_=w_grouped[quarter][:]
+                out=codes[:, cols].bitcast(FP8X4), scales=scales[:, cols], in_=w_grouped[(w_set, quarter)][:]
             )
 
         def first_conv(half, chunk):
@@ -262,40 +283,54 @@ def tile_butterflylayer2d_pb_t_kernel(tc, x_leaf, f_first, b_first, f_second, b_
             preparing = step < HALVES
             convolving = 1 <= step <= HALVES
             finishing = step >= 2
+            if convolving:
+                first_conv(step - 1, 0)
+                first_conv(step - 1, 1)
+            if preparing:
+                transpose_x(step, 0)
             if finishing:
                 regroup_h(step - 2, 1)
             if preparing:
-                regroup_w(step, 1)
-                transpose_x(step)
+                regroup_w(step, 0)
+                regroup_w_scalar(step, 1)
             if finishing:
                 quantise_h(step - 2, 1)
+            if convolving:
+                first_conv(step - 1, 2)
+                first_conv(step - 1, 3)
+            if preparing:
+                regroup_w(step, 2)
+                quantise_w(step, 0)
+            if finishing:
                 if step % 2 == 0:
                     spread_bias((step - 2) // 2)
                 second_conv(step - 2)
             if preparing:
-                regroup_w(step, 0)
-                regroup_w(step, 2)
-                quantise_w(step, 0)
-                quantise_x(step, 0)
-                quantise_w(step, 2)
-                quantise_x(step, 1)
-                quantise_w(step, 1)
-            if finishing:
-                add_bias(step - 2)
-            if convolving:
-                for chunk in range(4):
-                    first_conv(step - 1, chunk)
-            if finishing:
-                relu_and_store(step - 2)
-            if preparing:
-                regroup_w(step, 3)
-                if step + LOADS_AHEAD < HALVES:
-                    load(step + LOADS_AHEAD)
+                transpose_x(step, 1)
             if convolving:
                 regroup_h(step - 1, 0)
             if preparing:
-                quantise_w(step, 3)
+                quantise_w(step, 2)
+                quantise_x(step, 0)
+            if finishing:
+                add_bias(step - 2)
+            if convolving:
+                first_conv(step - 1, 4)
+                first_conv(step - 1, 5)
+            if preparing:
+                regroup_w_scalar(step, 3)
+                regroup_w(step, 3)
             if convolving:
                 quantise_h(step - 1, 0)
-                for chunk in range(4, CHUNKS):
-                    first_conv(step - 1, chunk)
+            if finishing:
+                relu_and_store(step - 2)
+            if preparing:
+                quantise_w(step, 1)
+                quantise_x(step, 1)
+            if convolving:
+                first_conv(step - 1, 6)
+                first_conv(step - 1, 7)
+            if preparing:
+                if step + LOADS_AHEAD < HALVES:
+                    load(step + LOADS_AHEAD)
+                quantise_w(step, 3)

@@ -24,6 +24,7 @@ QUARTER = 512
 SET_WORDS = 4 * QUARTER
 LOADS_AHEAD = 3
 SCALAR_PARTS = (0, 2, 0, 1)
+FIRST_SCALAR_PARTS = (0, 1, 0, 0)
 
 FLOPS = 2 * 4 * (1024 * 1024 * 1024 + 256 * 4096 * 256)
 
@@ -43,24 +44,27 @@ def tile_butterflylayer2d_pb_t_kernel(tc, x_leaf, f_first, b_first, f_second, b_
 
         identity = consts.tile([P, P], F32)
         make_identity(nc, identity[:])
+        identity_bf16 = consts.tile([P, P], BF16)
+        nc.gpsimd.tensor_copy(out=identity_bf16[:], in_=identity[:])
 
         warm = consts.tile([P, 1], F32)
         nc.gpsimd.memset(warm[:], 0.0)
         nc.scalar.activation(out=warm[:], in_=warm[:], func=RELU)
 
-        bias_first = consts.tile([P, 4 * CHUNKS], BF16)
-        with nc.allow_non_contiguous_dma(reason="a 8 KiB bias in runs of 4 values"):
-            nc.scalar.dma_start(
-                out=bias_first[:].rearrange("w (n lo) -> w n lo", lo=4),
-                in_=b_first.rearrange("i j (hi w lo) -> w (i j hi) lo", hi=2, lo=4),
-            )
         ones = consts.tile([P, P], BF16)
-        nc.gpsimd.memset(ones[:], 1.0)
-        bias_row = consts.tile([P, 4 * C_OUT], BF16)
-        nc.gpsimd.memset(bias_row[:], 0.0)
-        nc.scalar.dma_start(out=bias_row[0:1, :], in_=b_second.rearrange("(one i) j c -> one (i j c)", one=1))
+        nc.vector.memset(ones[:], 1.0)
+        rows_first = consts.tile([P, COLS], BF16)
+        nc.vector.memset(rows_first[:], 0.0)
+        row_second = consts.tile([P, 4 * C_OUT], BF16)
+        nc.vector.memset(row_second[:], 0.0)
+        nc.scalar.dma_start(out=rows_first[0:8, :], in_=b_first.rearrange("i j (hi c) -> (i j hi) c", hi=2))
+        nc.scalar.dma_start(out=row_second[0:1, :], in_=b_second.rearrange("(one i) j c -> one (i j c)", one=1))
+        bias_first = consts.tile([P, 4, 8], F32)
+        bias_second = consts.tile([P, 4 * C_OUT], F32)
 
         x_raw = {}
+        x_banks = {}
+        h_banks = {}
         w_raw = {}
         x_grouped = {}
         w_grouped = {}
@@ -69,7 +73,6 @@ def tile_butterflylayer2d_pb_t_kernel(tc, x_leaf, f_first, b_first, f_second, b_
         x_mx = {}
         w_mx = {}
         h_mx = {}
-        bias_second = {}
         acc_out = {}
         summed = {}
 
@@ -87,12 +90,7 @@ def tile_butterflylayer2d_pb_t_kernel(tc, x_leaf, f_first, b_first, f_second, b_
             i, j = divmod(half // 2, 2)
             rows = raw_pool.tile([P, RAW], BF16, tag="raw", name="w_rows")
             w_raw[(half, piece)] = rows
-            if half == 0:
-                source = f_first[i, j, piece].rearrange("q (c t) (h o) -> h (q c) t o", t=PACK, h=2)
-                for hi in range(2):
-                    part = rows[:, hi * RAW // 2 : (hi + 1) * RAW // 2]
-                    nc.sync.dma_start(out=part.rearrange("w (t o) -> w t o", t=PACK), in_=source[hi])
-            elif half % 2 == 0:
+            if half % 2 == 0:
                 nc.sync.dma_start(
                     out=rows[:],
                     in_=f_first[i, j, piece].rearrange("q (c t) o -> (q c) (t o)", t=PACK),
@@ -103,27 +101,40 @@ def tile_butterflylayer2d_pb_t_kernel(tc, x_leaf, f_first, b_first, f_second, b_
                     in_=f_second[i, j, piece].rearrange("q (hi w t) o -> w (q hi) (t o)", hi=2, t=PACK),
                 )
 
+        def load_first_w(piece, hi):
+            if (0, piece) not in w_raw:
+                w_raw[(0, piece)] = raw_pool.tile([P, RAW], BF16, tag="raw", name="w_rows")
+            part = w_raw[(0, piece)][:, hi * RAW // 2 : (hi + 1) * RAW // 2]
+            nc.sync.dma_start(
+                out=part.rearrange("w (t o) -> w t o", t=PACK),
+                in_=f_first[0, 0, piece].rearrange("q (c t) (h o) -> h (q c) t o", t=PACK, h=2)[hi],
+            )
+
         def load(half):
             load_w(half, 0)
+            load_w(half, 1)
             load_x(half, 0)
             load_x(half, 1)
-            load_w(half, 1)
 
         def transpose_x(half, p):
             words = x_raw[half][:].bitcast(F32)
-            grouped = grouped_pool.tile([P, PACK * COLS], BF16, tag="x_grouped", align_bytes=64)
-            x_grouped[(half, p)] = grouped
             for q2 in range(2):
                 bank = psum_x.tile([P, 4, P], F32, tag="x_bank")
+                x_banks[(half, p, q2)] = bank
                 for a in range(4):
                     x2, u = divmod(a, 2)
                     first = (8 * p + 2 * (2 * x2 + q2)) * P
                     nc.tensor.transpose(bank[:, a, :], words[:, first + u : first + 2 * P : 2], identity[:])
+
+        def copy_x(half, p):
+            grouped = grouped_pool.tile([P, PACK * COLS], BF16, tag="x_grouped", align_bytes=64)
+            x_grouped[(half, p)] = grouped
+            for q2 in range(2):
                 nc.scalar.copy(
                     out=grouped[:]
                     .bitcast(F32)
                     .rearrange("w (p2 q2 s a) -> w q2 p2 s a", p2=2, q2=2, a=4)[:, q2],
-                    in_=bank[:].rearrange("w a (s p2) -> w p2 s a", p2=2),
+                    in_=x_banks[(half, p, q2)][:].rearrange("w a (s p2) -> w p2 s a", p2=2),
                 )
 
         def quantise_x(half, p):
@@ -140,7 +151,7 @@ def tile_butterflylayer2d_pb_t_kernel(tc, x_leaf, f_first, b_first, f_second, b_
         def views_w(w_set, quarter):
             if (w_set, quarter) not in w_grouped:
                 w_grouped[(w_set, quarter)] = grouped_pool.tile(
-                    [P, PACK * QUARTER], BF16, tag="w_grouped", name="w_grouped", align_bytes=64
+                    [P, PACK * QUARTER], BF16, tag="w_grouped", name="w_grouped", align_bytes=64, bufs=6
                 )
             grouped = w_grouped[(w_set, quarter)]
             rows = w_raw[(w_set, quarter // 2)]
@@ -153,21 +164,24 @@ def tile_butterflylayer2d_pb_t_kernel(tc, x_leaf, f_first, b_first, f_second, b_
                 columns = grouped[:].rearrange("w (g c i t) -> w g c t i", g=2, i=4, t=PACK)
             return columns, source
 
+        def scalar_parts(w_set):
+            return SCALAR_PARTS if w_set > 1 else FIRST_SCALAR_PARTS
+
         def regroup_w_scalar(w_set, quarter):
             columns, source = views_w(w_set, quarter)
-            for part in range(SCALAR_PARTS[quarter]):
+            for part in range(scalar_parts(w_set)[quarter]):
                 nc.scalar.copy(out=columns[:, part], in_=source[:, part])
 
         def regroup_w(w_set, quarter):
             columns, source = views_w(w_set, quarter)
-            mine = SCALAR_PARTS[quarter]
+            mine = scalar_parts(w_set)[quarter]
             if mine == 0:
                 nc.vector.tensor_copy(out=columns, in_=source)
             elif mine == 1:
                 nc.vector.tensor_copy(out=columns[:, 1], in_=source[:, 1])
 
         def quantise_w(w_set, quarter):
-            if quarter == 0:
+            if w_set not in w_mx:
                 codes = set_pool.tile([P, SET_WORDS], U32, tag="w_codes", align_bytes=64)
                 scales = set_pool.tile([P, SET_WORDS], U8, tag="w_scales", align_bytes=64)
                 w_mx[w_set] = (codes, scales)
@@ -182,6 +196,7 @@ def tile_butterflylayer2d_pb_t_kernel(tc, x_leaf, f_first, b_first, f_second, b_
             w_codes, w_scales = w_mx[2 * node]
             x_codes, x_scales = x_mx[half]
             acc = psum_h.tile([P, COLS], F32, tag="acc_h")
+            h_banks[(half, chunk)] = acc
             for p in range(2):
                 w_cols = slice(p * C_MID + chunk * P, p * C_MID + (chunk + 1) * P)
                 x_cols = slice(p * COLS, (p + 1) * COLS)
@@ -194,15 +209,18 @@ def tile_butterflylayer2d_pb_t_kernel(tc, x_leaf, f_first, b_first, f_second, b_
                     start=(p == 0),
                     stop=(p == 1),
                 )
+
+        def relu_h(half, chunk):
+            node = half // 2
             if chunk % 4 == 0:
                 h_raw[(half, chunk // 4)] = grouped_pool.tile(
                     [P, 4 * COLS], BF16, tag="h_raw", name="h_raw", align_bytes=64
                 )
             nc.scalar.activation(
                 out=h_raw[(half, chunk // 4)][:, chunk % 4 * COLS : (chunk % 4 + 1) * COLS],
-                in_=acc[:],
+                in_=h_banks[(half, chunk)][:],
                 func=RELU,
-                bias=bias_first[:, node * CHUNKS + chunk : node * CHUNKS + chunk + 1],
+                bias=bias_first[:, chunk % 4, 2 * node + chunk // 4 : 2 * node + chunk // 4 + 1],
                 scale=1.0,
             )
 
@@ -227,17 +245,16 @@ def tile_butterflylayer2d_pb_t_kernel(tc, x_leaf, f_first, b_first, f_second, b_
                 in_=h_grouped[(half, group)][:],
             )
 
-        def spread_bias(node):
-            spread = psum_h.tile([P, COLS], F32, tag="acc_h")
-            nc.tensor.matmul(
-                out=spread[:, :C_OUT],
-                lhsT=ones[:],
-                rhs=bias_row[:, node * C_OUT : (node + 1) * C_OUT],
-                start=True,
-                stop=True,
-            )
-            bias_second[node] = out_pool.tile([P, C_OUT], F32, tag="bias_second", name="bias_second")
-            nc.scalar.copy(out=bias_second[node][:], in_=spread[:, :C_OUT])
+        def place_biases():
+            bank = psum_h.tile([P, 4, P], BF16, tag="acc_h")
+            for lo in range(4):
+                nc.tensor.transpose(bank[:, lo, :], rows_first[:, lo::4], identity_bf16[:])
+            nc.scalar.copy(out=bias_first[:], in_=bank[:, :, 0:8])
+            for part in range(2):
+                cols = slice(part * COLS, (part + 1) * COLS)
+                spread = psum_h.tile([P, COLS], F32, tag="acc_h")
+                nc.tensor.matmul(out=spread[:], lhsT=ones[:], rhs=row_second[:, cols], start=True, stop=True)
+                nc.scalar.copy(out=bias_second[:, cols], in_=spread[:])
 
         def second_conv(half):
             h_codes, h_scales = h_mx[half]
@@ -264,7 +281,7 @@ def tile_butterflylayer2d_pb_t_kernel(tc, x_leaf, f_first, b_first, f_second, b_
             nc.vector.tensor_tensor(
                 out=summed[half][:],
                 in0=acc_out[half][:],
-                in1=bias_second[node][:],
+                in1=bias_second[:, node * C_OUT : (node + 1) * C_OUT],
                 op=ADD,
             )
 
@@ -273,64 +290,124 @@ def tile_butterflylayer2d_pb_t_kernel(tc, x_leaf, f_first, b_first, f_second, b_
             first = (half % 2) * HALF_SAMPLES
             result = out_pool.tile([P, C_OUT], F32, tag="result")
             nc.scalar.activation(out=result[:], in_=summed[half][:], func=RELU)
-            nc.scalar.dma_start(
+            nc.sync.dma_start(
                 out=out[i, j, first : first + HALF_SAMPLES].rearrange("n y x c -> (n y x) c"), in_=result[:]
             )
 
-        for half in range(LOADS_AHEAD):
+        ctx.enter_context(tc.manual_schedule())
+        load_first_w(0, 0)
+        load_x(0, 0)
+        load_first_w(1, 0)
+        load_first_w(0, 1)
+        load_x(0, 1)
+        load_first_w(1, 1)
+        for half in range(1, LOADS_AHEAD):
             load(half)
-        for step in range(HALVES + 2):
-            preparing = step < HALVES
-            convolving = 1 <= step <= HALVES
+        regroup_w(0, 0)
+        quantise_w(0, 0)
+        transpose_x(0, 0)
+        copy_x(0, 0)
+        regroup_w(0, 2)
+        quantise_x(0, 0)
+        quantise_w(0, 2)
+        regroup_w_scalar(0, 1)
+        regroup_w(0, 1)
+        transpose_x(0, 1)
+        copy_x(0, 1)
+        place_biases()
+        regroup_w(0, 3)
+        quantise_w(0, 1)
+        quantise_x(0, 1)
+        for chunk in range(4):
+            first_conv(0, chunk)
+        quantise_w(0, 3)
+        regroup_w_scalar(1, 1)
+        load(LOADS_AHEAD)
+        for step in range(1, HALVES):
+            preparing = convolving = True
             finishing = step >= 2
-            if convolving:
-                first_conv(step - 1, 0)
-                first_conv(step - 1, 1)
             if preparing:
                 transpose_x(step, 0)
             if finishing:
-                regroup_h(step - 2, 1)
-            if preparing:
-                regroup_w(step, 0)
-                regroup_w_scalar(step, 1)
-            if finishing:
                 quantise_h(step - 2, 1)
             if convolving:
-                first_conv(step - 1, 2)
-                first_conv(step - 1, 3)
+                for chunk in range(4):
+                    relu_h(step - 1, chunk)
+                first_conv(step - 1, 4)
             if preparing:
+                regroup_w(step, 0)
                 regroup_w(step, 2)
-                quantise_w(step, 0)
             if finishing:
-                if step % 2 == 0:
-                    spread_bias((step - 2) // 2)
                 second_conv(step - 2)
             if preparing:
-                transpose_x(step, 1)
+                copy_x(step, 0)
             if convolving:
                 regroup_h(step - 1, 0)
             if preparing:
-                quantise_w(step, 2)
                 quantise_x(step, 0)
-            if finishing:
-                add_bias(step - 2)
             if convolving:
-                first_conv(step - 1, 4)
                 first_conv(step - 1, 5)
             if preparing:
-                regroup_w_scalar(step, 3)
-                regroup_w(step, 3)
+                transpose_x(step, 1)
             if convolving:
-                quantise_h(step - 1, 0)
-            if finishing:
-                relu_and_store(step - 2)
+                relu_h(step - 1, 4)
+                relu_h(step - 1, 5)
             if preparing:
-                quantise_w(step, 1)
-                quantise_x(step, 1)
+                copy_x(step, 1)
             if convolving:
                 first_conv(step - 1, 6)
                 first_conv(step - 1, 7)
+                quantise_h(step - 1, 0)
+            if finishing:
+                add_bias(step - 2)
+            if preparing:
+                quantise_x(step, 1)
+            if convolving:
+                relu_h(step - 1, 6)
+                relu_h(step - 1, 7)
+            if preparing:
+                quantise_w(step, 0)
+                regroup_w(step, 1)
+                quantise_w(step, 2)
+                if step < HALVES - 1:
+                    regroup_w(step, 3)
+                    quantise_w(step, 1)
+                for chunk in range(4):
+                    first_conv(step, chunk)
+            if convolving:
+                regroup_h(step - 1, 1)
+            if preparing:
+                if step < HALVES - 1:
+                    quantise_w(step, 3)
+                if step + 1 < HALVES:
+                    for quarter in range(4):
+                        regroup_w_scalar(step + 1, quarter)
+            if finishing:
+                relu_and_store(step - 2)
             if preparing:
                 if step + LOADS_AHEAD < HALVES:
                     load(step + LOADS_AHEAD)
-                quantise_w(step, 3)
+        last = HALVES - 1
+        quantise_h(last - 1, 1)
+        first_conv(last, 4)
+        relu_h(last, 0)
+        first_conv(last, 5)
+        relu_h(last, 1)
+        first_conv(last, 6)
+        relu_h(last, 2)
+        first_conv(last, 7)
+        for chunk in range(3, CHUNKS):
+            relu_h(last, chunk)
+        quantise_w(last, 1)
+        regroup_w(last, 3)
+        regroup_h(last, 0)
+        quantise_w(last, 3)
+        quantise_h(last, 0)
+        second_conv(last - 1)
+        add_bias(last - 1)
+        relu_and_store(last - 1)
+        regroup_h(last, 1)
+        quantise_h(last, 1)
+        second_conv(last)
+        add_bias(last)
+        relu_and_store(last)

@@ -173,12 +173,25 @@ def tile_butterflylayer2d_pb_t_kernel(tc, x_leaf, f_first, b_first, f_second, b_
                 nc.scalar.copy(out=columns[:, part], in_=source[:, part])
 
         def regroup_w(w_set, quarter):
-            columns, source = views_w(w_set, quarter)
+            views_w(w_set, quarter)
+            grouped = w_grouped[(w_set, quarter)]
+            rows = w_raw[(w_set, quarter // 2)]
             mine = scalar_parts(w_set)[quarter]
-            if mine == 0:
-                nc.vector.tensor_copy(out=columns, in_=source)
-            elif mine == 1:
-                nc.vector.tensor_copy(out=columns[:, 1], in_=source[:, 1])
+            if mine == 2:
+                return
+            if w_set % 2 == 0:
+                order = "w (h t c k i) -> w h c t k i" if w_set == 0 else "w (t h c k i) -> w h c t k i"
+                source = rows[:].rearrange(order, t=PACK, h=2, k=2, i=4)[:, quarter % 2]
+                columns = grouped[:].rearrange("w (i c k t) -> w c t k i", i=4, k=2, t=PACK)
+                first = 32 * mine
+                nc.vector.tensor_copy(out=columns[:, first:], in_=source[:, first:])
+            else:
+                source = rows[:].rearrange("w (h g t c i) -> w h g c t i", h=2, g=2, t=PACK, i=8)[:, quarter % 2]
+                columns = grouped[:].rearrange("w (g c i t) -> w g c t i", g=2, i=8, t=PACK)
+                if mine == 0:
+                    nc.vector.tensor_copy(out=columns, in_=source)
+                else:
+                    nc.vector.tensor_copy(out=columns[:, 1], in_=source[:, 1])
 
         def quantise_w(w_set, quarter):
             if w_set not in w_mx:
@@ -228,8 +241,8 @@ def tile_butterflylayer2d_pb_t_kernel(tc, x_leaf, f_first, b_first, f_second, b_
             grouped = grouped_pool.tile([P, PACK * COLS], BF16, tag="h_grouped", align_bytes=64)
             h_grouped[(half, group)] = grouped
             nc.vector.tensor_copy(
-                out=grouped[:].rearrange("w (c i t) -> w c t i", i=4, t=PACK),
-                in_=h_raw[(half, group)][:].rearrange("w (t c i) -> w c t i", t=PACK, i=4),
+                out=grouped[:].rearrange("w (c i t) -> w c t i", i=8, t=PACK),
+                in_=h_raw[(half, group)][:].rearrange("w (t c i) -> w c t i", t=PACK, i=8),
             )
 
         def quantise_h(half, group):

@@ -112,8 +112,8 @@ def tile_butterflylayer2d_pb_t_kernel(tc, x_leaf, f_first, b_first, f_second, b_
 
         def load(half):
             load_w(half, 0)
-            load_w(half, 1)
             load_x(half, 0)
+            load_w(half, 1)
             load_x(half, 1)
 
         def transpose_x(half, p):
@@ -156,42 +156,27 @@ def tile_butterflylayer2d_pb_t_kernel(tc, x_leaf, f_first, b_first, f_second, b_
             grouped = w_grouped[(w_set, quarter)]
             rows = w_raw[(w_set, quarter // 2)]
             if w_set % 2 == 0:
-                order = "w (h t g c i) -> w h g c t i" if w_set == 0 else "w (t h g c i) -> w h g c t i"
-                source = rows[:].rearrange(order, t=PACK, h=2, g=2, i=4)[:, quarter % 2]
-                columns = grouped[:].rearrange("w (i g c t) -> w g c t i", i=4, g=2, t=PACK)
-            else:
-                source = rows[:].rearrange("w (h g t c i) -> w h g c t i", h=2, g=2, t=PACK, i=4)[:, quarter % 2]
-                columns = grouped[:].rearrange("w (g c i t) -> w g c t i", g=2, i=4, t=PACK)
-            return columns, source
+                order = "w (h t c k i) -> w h c t k i" if w_set == 0 else "w (t h c k i) -> w h c t k i"
+                source = rows[:].rearrange(order, t=PACK, h=2, k=2, i=4)[:, quarter % 2]
+                columns = grouped[:].rearrange("w (i c k t) -> w c t k i", i=4, k=2, t=PACK)
+                return [(columns[:, half], source[:, half]) for half in (slice(0, 32), slice(32, 64), slice(0, 64))]
+            source = rows[:].rearrange("w (h g t c i) -> w h g c t i", h=2, g=2, t=PACK, i=8)[:, quarter % 2]
+            columns = grouped[:].rearrange("w (g c i t) -> w g c t i", g=2, i=8, t=PACK)
+            return [(columns[:, 0], source[:, 0]), (columns[:, 1], source[:, 1]), (columns, source)]
 
         def scalar_parts(w_set):
             return SCALAR_PARTS if w_set > 1 else FIRST_SCALAR_PARTS
 
         def regroup_w_scalar(w_set, quarter):
-            columns, source = views_w(w_set, quarter)
-            for part in range(scalar_parts(w_set)[quarter]):
-                nc.scalar.copy(out=columns[:, part], in_=source[:, part])
+            views = views_w(w_set, quarter)
+            for columns, source in views[: scalar_parts(w_set)[quarter]]:
+                nc.scalar.copy(out=columns, in_=source)
 
         def regroup_w(w_set, quarter):
-            views_w(w_set, quarter)
-            grouped = w_grouped[(w_set, quarter)]
-            rows = w_raw[(w_set, quarter // 2)]
             mine = scalar_parts(w_set)[quarter]
-            if mine == 2:
-                return
-            if w_set % 2 == 0:
-                order = "w (h t c k i) -> w h c t k i" if w_set == 0 else "w (t h c k i) -> w h c t k i"
-                source = rows[:].rearrange(order, t=PACK, h=2, k=2, i=4)[:, quarter % 2]
-                columns = grouped[:].rearrange("w (i c k t) -> w c t k i", i=4, k=2, t=PACK)
-                first = 32 * mine
-                nc.vector.tensor_copy(out=columns[:, first:], in_=source[:, first:])
-            else:
-                source = rows[:].rearrange("w (h g t c i) -> w h g c t i", h=2, g=2, t=PACK, i=8)[:, quarter % 2]
-                columns = grouped[:].rearrange("w (g c i t) -> w g c t i", g=2, i=8, t=PACK)
-                if mine == 0:
-                    nc.vector.tensor_copy(out=columns, in_=source)
-                else:
-                    nc.vector.tensor_copy(out=columns[:, 1], in_=source[:, 1])
+            if mine < 2:
+                columns, source = views_w(w_set, quarter)[2 if mine == 0 else 1]
+                nc.vector.tensor_copy(out=columns, in_=source)
 
         def quantise_w(w_set, quarter):
             if w_set not in w_mx:
@@ -225,7 +210,7 @@ def tile_butterflylayer2d_pb_t_kernel(tc, x_leaf, f_first, b_first, f_second, b_
 
         def relu_h(half, chunk):
             node = half // 2
-            if chunk % 4 == 0:
+            if (half, chunk // 4) not in h_raw:
                 h_raw[(half, chunk // 4)] = grouped_pool.tile(
                     [P, 4 * COLS], BF16, tag="h_raw", name="h_raw", align_bytes=64
                 )
@@ -237,25 +222,28 @@ def tile_butterflylayer2d_pb_t_kernel(tc, x_leaf, f_first, b_first, f_second, b_
                 scale=1.0,
             )
 
-        def regroup_h(half, group):
-            grouped = grouped_pool.tile([P, PACK * COLS], BF16, tag="h_grouped", align_bytes=64)
-            h_grouped[(half, group)] = grouped
+        def regroup_h(half, group, part=slice(0, COLS)):
+            if (half, group) not in h_grouped:
+                h_grouped[(half, group)] = grouped_pool.tile(
+                    [P, PACK * COLS], BF16, tag="h_grouped", name="h_grouped", align_bytes=64
+                )
+            runs = slice(part.start // 8, part.stop // 8)
             nc.vector.tensor_copy(
-                out=grouped[:].rearrange("w (c i t) -> w c t i", i=8, t=PACK),
-                in_=h_raw[(half, group)][:].rearrange("w (t c i) -> w c t i", t=PACK, i=8),
+                out=h_grouped[(half, group)][:].rearrange("w (c i t) -> w c t i", i=8, t=PACK)[:, runs],
+                in_=h_raw[(half, group)][:].rearrange("w (t c i) -> w c t i", t=PACK, i=8)[:, runs],
             )
 
-        def quantise_h(half, group):
-            if group == 0:
+        def quantise_h(half, group, part=slice(0, COLS)):
+            if half not in h_mx:
                 codes = code_pool.tile([P, CHUNKS * P], U32, tag="h_codes", align_bytes=64)
                 scales = code_pool.tile([P, CHUNKS * P], U8, tag="h_scales", align_bytes=64)
                 h_mx[half] = (codes, scales)
             codes, scales = h_mx[half]
-            cols = slice(group * 4 * P, (group + 1) * 4 * P)
+            cols = slice(group * COLS + part.start, group * COLS + part.stop)
             nc.vector.quantize_mx(
                 out=codes[:, cols].bitcast(FP8X4),
                 scales=scales[:, cols],
-                in_=h_grouped[(half, group)][:],
+                in_=h_grouped[(half, group)][:, PACK * part.start : PACK * part.stop],
             )
 
         def place_biases():
@@ -269,12 +257,14 @@ def tile_butterflylayer2d_pb_t_kernel(tc, x_leaf, f_first, b_first, f_second, b_
                 nc.tensor.matmul(out=spread[:], lhsT=ones[:], rhs=row_second[:, cols], start=True, stop=True)
                 nc.scalar.copy(out=bias_second[:, cols], in_=spread[:])
 
-        def second_conv(half):
+        def second_conv(half, chunks=range(CHUNKS)):
             h_codes, h_scales = h_mx[half]
             w_codes, w_scales = w_mx[2 * (half // 2) + 1]
-            acc = psum_out.tile([P, C_OUT], F32, tag="acc_out")
-            acc_out[half] = acc
-            for chunk in range(CHUNKS):
+            if half not in acc_out:
+                pool, tag = (psum_x, "x_bank") if half == HALVES - 1 else (psum_out, "acc_out")
+                acc_out[half] = pool.tile([P, C_OUT], F32, tag=tag, name="acc_out")
+            acc = acc_out[half]
+            for chunk in chunks:
                 hi, place = divmod(chunk, 4)
                 h_cols = slice(chunk * P, (chunk + 1) * P)
                 w_cols = slice((2 * place + hi) * C_OUT, (2 * place + hi + 1) * C_OUT)
@@ -288,23 +278,24 @@ def tile_butterflylayer2d_pb_t_kernel(tc, x_leaf, f_first, b_first, f_second, b_
                     stop=(chunk == CHUNKS - 1),
                 )
 
-        def add_bias(half):
+        def add_bias(half, cols=slice(0, C_OUT)):
             node = half // 2
-            summed[half] = out_pool.tile([P, C_OUT], F32, tag="summed", name="summed")
+            if half not in summed:
+                summed[half] = out_pool.tile([P, C_OUT], F32, tag="summed", name="summed")
             nc.vector.tensor_tensor(
-                out=summed[half][:],
-                in0=acc_out[half][:],
-                in1=bias_second[:, node * C_OUT : (node + 1) * C_OUT],
+                out=summed[half][:, cols],
+                in0=acc_out[half][:, cols],
+                in1=bias_second[:, node * C_OUT + cols.start : node * C_OUT + cols.stop],
                 op=ADD,
             )
 
-        def relu_and_store(half):
+        def relu_and_store(half, cols=slice(0, C_OUT)):
             i, j = divmod(half // 2, 2)
             first = (half % 2) * HALF_SAMPLES
-            result = out_pool.tile([P, C_OUT], F32, tag="result")
-            nc.scalar.activation(out=result[:], in_=summed[half][:], func=RELU)
+            result = out_pool.tile([P, cols.stop - cols.start], F32, tag="result")
+            nc.scalar.activation(out=result[:], in_=summed[half][:, cols], func=RELU)
             nc.sync.dma_start(
-                out=out[i, j, first : first + HALF_SAMPLES].rearrange("n y x c -> (n y x) c"), in_=result[:]
+                out=out[i, j, first : first + HALF_SAMPLES].rearrange("n y x c -> (n y x) c")[:, cols], in_=result[:]
             )
 
         ctx.enter_context(tc.manual_schedule())
@@ -344,7 +335,7 @@ def tile_butterflylayer2d_pb_t_kernel(tc, x_leaf, f_first, b_first, f_second, b_
             if finishing:
                 quantise_h(step - 2, 1)
             if convolving:
-                for chunk in range(4):
+                for chunk in (1, 0, 3, 2):
                     relu_h(step - 1, chunk)
                 first_conv(step - 1, 4)
             if preparing:
@@ -363,8 +354,8 @@ def tile_butterflylayer2d_pb_t_kernel(tc, x_leaf, f_first, b_first, f_second, b_
             if preparing:
                 transpose_x(step, 1)
             if convolving:
-                relu_h(step - 1, 4)
                 relu_h(step - 1, 5)
+                relu_h(step - 1, 4)
             if preparing:
                 copy_x(step, 1)
             if convolving:
@@ -373,15 +364,14 @@ def tile_butterflylayer2d_pb_t_kernel(tc, x_leaf, f_first, b_first, f_second, b_
                 quantise_h(step - 1, 0)
             if finishing:
                 add_bias(step - 2)
-            if preparing:
-                quantise_x(step, 1)
             if convolving:
-                relu_h(step - 1, 6)
                 relu_h(step - 1, 7)
+                relu_h(step - 1, 6)
             if preparing:
                 quantise_w(step, 0)
                 regroup_w(step, 1)
                 quantise_w(step, 2)
+                quantise_x(step, 1)
                 if step < HALVES - 1:
                     regroup_w(step, 3)
                     quantise_w(step, 1)
@@ -401,26 +391,33 @@ def tile_butterflylayer2d_pb_t_kernel(tc, x_leaf, f_first, b_first, f_second, b_
                 if step + LOADS_AHEAD < HALVES:
                     load(step + LOADS_AHEAD)
         last = HALVES - 1
+        left, right = slice(0, COLS // 2), slice(COLS // 2, COLS)
         quantise_h(last - 1, 1)
         first_conv(last, 4)
+        relu_h(last, 1)
         relu_h(last, 0)
         first_conv(last, 5)
-        relu_h(last, 1)
         first_conv(last, 6)
+        relu_h(last, 3)
         relu_h(last, 2)
         first_conv(last, 7)
-        for chunk in range(3, CHUNKS):
+        for chunk in range(4, CHUNKS):
             relu_h(last, chunk)
         quantise_w(last, 1)
         regroup_w(last, 3)
         regroup_h(last, 0)
         quantise_w(last, 3)
-        quantise_h(last, 0)
         second_conv(last - 1)
+        quantise_h(last, 0)
+        second_conv(last, range(4))
+        regroup_h(last, 1, left)
+        regroup_h(last, 1, right)
         add_bias(last - 1)
         relu_and_store(last - 1)
-        regroup_h(last, 1)
-        quantise_h(last, 1)
-        second_conv(last)
-        add_bias(last)
-        relu_and_store(last)
+        quantise_h(last, 1, left)
+        second_conv(last, range(4, 6))
+        quantise_h(last, 1, right)
+        second_conv(last, range(6, 8))
+        for cols in (slice(0, P), slice(P, C_OUT)):
+            add_bias(last, cols)
+            relu_and_store(last, cols)

@@ -23,7 +23,7 @@ RAW = 4096
 QUARTER = 512
 SET_WORDS = 4 * QUARTER
 LOADS_AHEAD = 3
-SCALAR_PARTS = (0, 2, 0, 1)
+SCALAR_PARTS = ((0, 2, 0, 1), (0, 2, 0, 0))
 FIRST_SCALAR_PARTS = (0, 1, 0, 0)
 
 FLOPS = 2 * 4 * (1024 * 1024 * 1024 + 256 * 4096 * 256)
@@ -156,27 +156,42 @@ def tile_butterflylayer2d_pb_t_kernel(tc, x_leaf, f_first, b_first, f_second, b_
             grouped = w_grouped[(w_set, quarter)]
             rows = w_raw[(w_set, quarter // 2)]
             if w_set % 2 == 0:
+                order = "w (h t g c i) -> w h g c t i" if w_set == 0 else "w (t h g c i) -> w h g c t i"
+                source = rows[:].rearrange(order, t=PACK, h=2, g=2, i=4)[:, quarter % 2]
+                columns = grouped[:].rearrange("w (i g c t) -> w g c t i", i=4, g=2, t=PACK)
+            else:
+                source = rows[:].rearrange("w (h g t c i) -> w h g c t i", h=2, g=2, t=PACK, i=4)[:, quarter % 2]
+                columns = grouped[:].rearrange("w (g c i t) -> w g c t i", g=2, i=4, t=PACK)
+            return columns, source
+
+        def scalar_parts(w_set):
+            return SCALAR_PARTS[w_set % 2] if w_set > 1 else FIRST_SCALAR_PARTS
+
+        def regroup_w_scalar(w_set, quarter):
+            columns, source = views_w(w_set, quarter)
+            for part in range(scalar_parts(w_set)[quarter]):
+                nc.scalar.copy(out=columns[:, part], in_=source[:, part])
+
+        def regroup_w(w_set, quarter):
+            views_w(w_set, quarter)
+            grouped = w_grouped[(w_set, quarter)]
+            rows = w_raw[(w_set, quarter // 2)]
+            mine = scalar_parts(w_set)[quarter]
+            if mine == 2:
+                return
+            if w_set % 2 == 0:
                 order = "w (h t c k i) -> w h c t k i" if w_set == 0 else "w (t h c k i) -> w h c t k i"
                 source = rows[:].rearrange(order, t=PACK, h=2, k=2, i=4)[:, quarter % 2]
                 columns = grouped[:].rearrange("w (i c k t) -> w c t k i", i=4, k=2, t=PACK)
-                return [(columns[:, half], source[:, half]) for half in (slice(0, 32), slice(32, 64), slice(0, 64))]
-            source = rows[:].rearrange("w (h g t c i) -> w h g c t i", h=2, g=2, t=PACK, i=8)[:, quarter % 2]
-            columns = grouped[:].rearrange("w (g c i t) -> w g c t i", g=2, i=8, t=PACK)
-            return [(columns[:, 0], source[:, 0]), (columns[:, 1], source[:, 1]), (columns, source)]
-
-        def scalar_parts(w_set):
-            return SCALAR_PARTS if w_set > 1 else FIRST_SCALAR_PARTS
-
-        def regroup_w_scalar(w_set, quarter):
-            views = views_w(w_set, quarter)
-            for columns, source in views[: scalar_parts(w_set)[quarter]]:
-                nc.scalar.copy(out=columns, in_=source)
-
-        def regroup_w(w_set, quarter):
-            mine = scalar_parts(w_set)[quarter]
-            if mine < 2:
-                columns, source = views_w(w_set, quarter)[2 if mine == 0 else 1]
-                nc.vector.tensor_copy(out=columns, in_=source)
+                first = 32 * mine
+                nc.vector.tensor_copy(out=columns[:, first:], in_=source[:, first:])
+            else:
+                source = rows[:].rearrange("w (h g t c i) -> w h g c t i", h=2, g=2, t=PACK, i=8)[:, quarter % 2]
+                columns = grouped[:].rearrange("w (g c i t) -> w g c t i", g=2, i=8, t=PACK)
+                if mine == 0:
+                    nc.vector.tensor_copy(out=columns, in_=source)
+                else:
+                    nc.vector.tensor_copy(out=columns[:, 1], in_=source[:, 1])
 
         def quantise_w(w_set, quarter):
             if w_set not in w_mx:
@@ -193,8 +208,9 @@ def tile_butterflylayer2d_pb_t_kernel(tc, x_leaf, f_first, b_first, f_second, b_
             node = half // 2
             w_codes, w_scales = w_mx[2 * node]
             x_codes, x_scales = x_mx[half]
-            acc = psum_h.tile([P, COLS], F32, tag="acc_h")
-            h_banks[(half, chunk)] = acc
+            if (half, chunk) not in h_banks:
+                h_banks[(half, chunk)] = psum_h.tile([P, COLS], F32, tag="acc_h", name="acc_h")
+            acc = h_banks[(half, chunk)]
             for p in range(2):
                 w_cols = slice(p * C_MID + chunk * P, p * C_MID + (chunk + 1) * P)
                 x_cols = slice(p * COLS, (p + 1) * COLS)
@@ -206,6 +222,18 @@ def tile_butterflylayer2d_pb_t_kernel(tc, x_leaf, f_first, b_first, f_second, b_
                     rhs_scale=x_scales[:, x_cols],
                     start=(p == 0),
                     stop=(p == 1),
+                )
+
+        def keep_warm(half, p):
+            if (half, 0) not in h_banks:
+                h_banks[(half, 0)] = psum_h.tile([P, COLS], F32, tag="acc_h", name="acc_h")
+            for run in range(2):
+                nc.tensor.matmul(
+                    out=h_banks[(half, 0)][:],
+                    lhsT=identity_bf16[:],
+                    rhs=x_grouped[(half, p)][:, run * COLS : (run + 1) * COLS],
+                    start=True,
+                    stop=True,
                 )
 
         def relu_h(half, chunk):
@@ -335,7 +363,7 @@ def tile_butterflylayer2d_pb_t_kernel(tc, x_leaf, f_first, b_first, f_second, b_
             if finishing:
                 quantise_h(step - 2, 1)
             if convolving:
-                for chunk in (1, 0, 3, 2):
+                for chunk in range(4):
                     relu_h(step - 1, chunk)
                 first_conv(step - 1, 4)
             if preparing:
@@ -350,23 +378,25 @@ def tile_butterflylayer2d_pb_t_kernel(tc, x_leaf, f_first, b_first, f_second, b_
             if preparing:
                 quantise_x(step, 0)
             if convolving:
-                first_conv(step - 1, 5)
+                for chunk in (5, 6, 7):
+                    first_conv(step - 1, chunk)
             if preparing:
                 transpose_x(step, 1)
+                keep_warm(step, 0)
             if convolving:
-                relu_h(step - 1, 5)
                 relu_h(step - 1, 4)
+                relu_h(step - 1, 5)
             if preparing:
                 copy_x(step, 1)
+            if preparing:
+                keep_warm(step, 1)
             if convolving:
-                first_conv(step - 1, 6)
-                first_conv(step - 1, 7)
                 quantise_h(step - 1, 0)
             if finishing:
                 add_bias(step - 2)
             if convolving:
-                relu_h(step - 1, 7)
                 relu_h(step - 1, 6)
+                relu_h(step - 1, 7)
             if preparing:
                 quantise_w(step, 0)
                 regroup_w(step, 1)

@@ -23,8 +23,9 @@ RAW = 4096
 QUARTER = 512
 SET_WORDS = 4 * QUARTER
 LOADS_AHEAD = 3
-SCALAR_PARTS = ((0, 2, 0, 1), (0, 2, 0, 0))
-FIRST_SCALAR_PARTS = (0, 1, 0, 0)
+WARM_UP = 24
+SCALAR_PARTS = ((0, 2, 0, 1), (0, 2, 0, 1))
+FIRST_SCALAR_PARTS = ((0, 0, 0, 0), (0, 2, 0, 0))
 
 FLOPS = 2 * 4 * (1024 * 1024 * 1024 + 256 * 4096 * 256)
 
@@ -37,7 +38,7 @@ def tile_butterflylayer2d_pb_t_kernel(tc, x_leaf, f_first, b_first, f_second, b_
         grouped_pool = ctx.enter_context(tc.tile_pool(name="grouped", bufs=4))
         set_pool = ctx.enter_context(tc.tile_pool(name="sets", bufs=3))
         code_pool = ctx.enter_context(tc.tile_pool(name="codes", bufs=2))
-        out_pool = ctx.enter_context(tc.tile_pool(name="outs", bufs=2))
+        out_pool = ctx.enter_context(tc.tile_pool(name="outs", bufs=3))
         psum_x = ctx.enter_context(tc.psum_pool(name="psum_x", bufs=2))
         psum_h = ctx.enter_context(tc.psum_pool(name="psum_h", bufs=5))
         psum_out = ctx.enter_context(tc.psum_pool(name="psum_out", bufs=1))
@@ -148,24 +149,28 @@ def tile_butterflylayer2d_pb_t_kernel(tc, x_leaf, f_first, b_first, f_second, b_
                 out=codes[:, cols].bitcast(FP8X4), scales=scales[:, cols], in_=x_grouped[(half, p)][:]
             )
 
-        def views_w(w_set, quarter):
-            if (w_set, quarter) not in w_grouped:
-                w_grouped[(w_set, quarter)] = grouped_pool.tile(
-                    [P, PACK * QUARTER], BF16, tag="w_grouped", name="w_grouped", align_bytes=64, bufs=6
+        def grouped_w(w_set, quarter):
+            piece = quarter // 2
+            if (w_set, piece) not in w_grouped:
+                w_grouped[(w_set, piece)] = grouped_pool.tile(
+                    [P, RAW], BF16, tag="w_grouped", name="w_grouped", align_bytes=64, bufs=5
                 )
-            grouped = w_grouped[(w_set, quarter)]
+            return w_grouped[(w_set, piece)][:, quarter % 2 * PACK * QUARTER : (quarter % 2 + 1) * PACK * QUARTER]
+
+        def views_w(w_set, quarter):
+            grouped = grouped_w(w_set, quarter)
             rows = w_raw[(w_set, quarter // 2)]
             if w_set % 2 == 0:
                 order = "w (h t g c i) -> w h g c t i" if w_set == 0 else "w (t h g c i) -> w h g c t i"
                 source = rows[:].rearrange(order, t=PACK, h=2, g=2, i=4)[:, quarter % 2]
-                columns = grouped[:].rearrange("w (i g c t) -> w g c t i", i=4, g=2, t=PACK)
+                columns = grouped.rearrange("w (i g c t) -> w g c t i", i=4, g=2, t=PACK)
             else:
                 source = rows[:].rearrange("w (h g t c i) -> w h g c t i", h=2, g=2, t=PACK, i=4)[:, quarter % 2]
-                columns = grouped[:].rearrange("w (g c i t) -> w g c t i", g=2, i=4, t=PACK)
+                columns = grouped.rearrange("w (g c i t) -> w g c t i", g=2, i=4, t=PACK)
             return columns, source
 
         def scalar_parts(w_set):
-            return SCALAR_PARTS[w_set % 2] if w_set > 1 else FIRST_SCALAR_PARTS
+            return SCALAR_PARTS[w_set % 2] if w_set > 1 else FIRST_SCALAR_PARTS[w_set]
 
         def regroup_w_scalar(w_set, quarter):
             columns, source = views_w(w_set, quarter)
@@ -173,8 +178,7 @@ def tile_butterflylayer2d_pb_t_kernel(tc, x_leaf, f_first, b_first, f_second, b_
                 nc.scalar.copy(out=columns[:, part], in_=source[:, part])
 
         def regroup_w(w_set, quarter):
-            views_w(w_set, quarter)
-            grouped = w_grouped[(w_set, quarter)]
+            grouped = grouped_w(w_set, quarter)
             rows = w_raw[(w_set, quarter // 2)]
             mine = scalar_parts(w_set)[quarter]
             if mine == 2:
@@ -182,26 +186,29 @@ def tile_butterflylayer2d_pb_t_kernel(tc, x_leaf, f_first, b_first, f_second, b_
             if w_set % 2 == 0:
                 order = "w (h t c k i) -> w h c t k i" if w_set == 0 else "w (t h c k i) -> w h c t k i"
                 source = rows[:].rearrange(order, t=PACK, h=2, k=2, i=4)[:, quarter % 2]
-                columns = grouped[:].rearrange("w (i c k t) -> w c t k i", i=4, k=2, t=PACK)
+                columns = grouped.rearrange("w (i c k t) -> w c t k i", i=4, k=2, t=PACK)
                 first = 32 * mine
                 nc.vector.tensor_copy(out=columns[:, first:], in_=source[:, first:])
             else:
                 source = rows[:].rearrange("w (h g t c i) -> w h g c t i", h=2, g=2, t=PACK, i=8)[:, quarter % 2]
-                columns = grouped[:].rearrange("w (g c i t) -> w g c t i", g=2, i=8, t=PACK)
+                columns = grouped.rearrange("w (g c i t) -> w g c t i", g=2, i=8, t=PACK)
                 if mine == 0:
                     nc.vector.tensor_copy(out=columns, in_=source)
                 else:
                     nc.vector.tensor_copy(out=columns[:, 1], in_=source[:, 1])
 
-        def quantise_w(w_set, quarter):
+        def quantise_w(w_set, quarter, count=1):
             if w_set not in w_mx:
                 codes = set_pool.tile([P, SET_WORDS], U32, tag="w_codes", align_bytes=64)
                 scales = set_pool.tile([P, SET_WORDS], U8, tag="w_scales", align_bytes=64)
                 w_mx[w_set] = (codes, scales)
             codes, scales = w_mx[w_set]
-            cols = slice(quarter * QUARTER, (quarter + 1) * QUARTER)
+            cols = slice(quarter * QUARTER, (quarter + count) * QUARTER)
+            first = quarter % 2 * PACK * QUARTER
             nc.vector.quantize_mx(
-                out=codes[:, cols].bitcast(FP8X4), scales=scales[:, cols], in_=w_grouped[(w_set, quarter)][:]
+                out=codes[:, cols].bitcast(FP8X4),
+                scales=scales[:, cols],
+                in_=w_grouped[(w_set, quarter // 2)][:, first : first + count * PACK * QUARTER],
             )
 
         def first_conv(half, chunk):
@@ -235,6 +242,11 @@ def tile_butterflylayer2d_pb_t_kernel(tc, x_leaf, f_first, b_first, f_second, b_
                     start=True,
                     stop=True,
                 )
+
+        def warm_up():
+            h_banks[(0, 0)] = psum_h.tile([P, COLS], F32, tag="acc_h", name="acc_h")
+            for turn in range(WARM_UP):
+                nc.tensor.matmul(out=h_banks[(0, 0)][:, :P], lhsT=ones[:], rhs=ones[:], start=True, stop=True)
 
         def relu_h(half, chunk):
             node = half // 2
@@ -335,23 +347,24 @@ def tile_butterflylayer2d_pb_t_kernel(tc, x_leaf, f_first, b_first, f_second, b_
         load_first_w(1, 1)
         for half in range(1, LOADS_AHEAD):
             load(half)
+        warm_up()
         regroup_w(0, 0)
         quantise_w(0, 0)
         transpose_x(0, 0)
         copy_x(0, 0)
+        place_biases()
         regroup_w(0, 2)
         quantise_x(0, 0)
         quantise_w(0, 2)
-        regroup_w_scalar(0, 1)
         regroup_w(0, 1)
         transpose_x(0, 1)
         copy_x(0, 1)
-        place_biases()
+        keep_warm(0, 1)
         regroup_w(0, 3)
-        quantise_w(0, 1)
         quantise_x(0, 1)
         for chunk in range(4):
             first_conv(0, chunk)
+        quantise_w(0, 1)
         quantise_w(0, 3)
         regroup_w_scalar(1, 1)
         load(LOADS_AHEAD)

from contextlib import ExitStack

import concourse.mybir as mybir
from concourse.masks import make_identity

BF16 = mybir.dt.bfloat16
F32 = mybir.dt.float32
U32 = mybir.dt.uint32
U8 = mybir.dt.uint8
FP8X4 = mybir.dt.float8_e4m3fn_x4
RELU = mybir.ActivationFunctionType.Relu
ADD = mybir.AluOpType.add

P = 128
PACK = 4
HALVES = 8
HALF_SAMPLES = 32
C_MID = 1024
C_OUT = 256
CHUNKS = C_MID // P
COLS = 512
RAW = 4096
QUARTER = 512
SET_WORDS = 4 * QUARTER
LOADS_AHEAD = 3
WARM_UP = 24
SCALAR_PARTS = ((0, 2, 0, 1), (0, 2, 0, 1))
FIRST_SCALAR_PARTS = ((0, 0, 0, 0), (0, 2, 0, 0))

FLOPS = 2 * 4 * (1024 * 1024 * 1024 + 256 * 4096 * 256)


def tile_butterflylayer2d_pb_t_kernel(tc, x_leaf, f_first, b_first, f_second, b_second, out):
    nc = tc.nc
    with ExitStack() as ctx:
        consts = ctx.enter_context(tc.tile_pool(name="consts", bufs=1))
        raw_pool = ctx.enter_context(tc.tile_pool(name="raw", bufs=3 * LOADS_AHEAD))
        grouped_pool = ctx.enter_context(tc.tile_pool(name="grouped", bufs=4))
        set_pool = ctx.enter_context(tc.tile_pool(name="sets", bufs=3))
        code_pool = ctx.enter_context(tc.tile_pool(name="codes", bufs=2))
        out_pool = ctx.enter_context(tc.tile_pool(name="outs", bufs=3))
        psum_x = ctx.enter_context(tc.psum_pool(name="psum_x", bufs=2))
        psum_h = ctx.enter_context(tc.psum_pool(name="psum_h", bufs=5))
        psum_out = ctx.enter_context(tc.psum_pool(name="psum_out", bufs=1))

        identity = consts.tile([P, P], F32)
        make_identity(nc, identity[:])
        identity_bf16 = consts.tile([P, P], BF16)
        nc.gpsimd.tensor_copy(out=identity_bf16[:], in_=identity[:])

        warm = consts.tile([P, 1], F32)
        nc.gpsimd.memset(warm[:], 0.0)
        nc.scalar.activation(out=warm[:], in_=warm[:], func=RELU)

        ones = consts.tile([P, P], BF16)
        nc.vector.memset(ones[:], 1.0)
        rows_first = consts.tile([P, COLS], BF16)
        nc.vector.memset(rows_first[:], 0.0)
        row_second = consts.tile([P, 4 * C_OUT], BF16)
        nc.vector.memset(row_second[:], 0.0)
        nc.scalar.dma_start(out=rows_first[0:8, :], in_=b_first.rearrange("i j (hi c) -> (i j hi) c", hi=2))
        nc.scalar.dma_start(out=row_second[0:1, :], in_=b_second.rearrange("(one i) j c -> one (i j c)", one=1))
        bias_first = consts.tile([P, 4, 8], F32)
        bias_second = consts.tile([P, 4 * C_OUT], F32)

        x_raw = {}
        x_banks = {}
        h_banks = {}
        w_raw = {}
        x_grouped = {}
        w_grouped = {}
        h_raw = {}
        h_grouped = {}
        x_mx = {}
        w_mx = {}
        h_mx = {}
        acc_out = {}
        summed = {}

        def load_x(half, p):
            i, j = divmod(half // 2, 2)
            first = (half % 2) * HALF_SAMPLES
            if p == 0:
                x_raw[half] = raw_pool.tile([P, RAW], BF16, tag="raw", name="x_rows")
            nc.sync.dma_start(
                out=x_raw[half][:, p * RAW // 2 : (p + 1) * RAW // 2],
                in_=x_leaf[i, j, first : first + HALF_SAMPLES].rearrange("n (yh p) x c -> p (n yh) (x c)", p=2)[p],
            )

        def load_w(half, piece):
            i, j = divmod(half // 2, 2)
            rows = raw_pool.tile([P, RAW], BF16, tag="raw", name="w_rows")
            w_raw[(half, piece)] = rows
            if half % 2 == 0:
                nc.sync.dma_start(
                    out=rows[:],
                    in_=f_first[i, j, piece].rearrange("q (c t) o -> (q c) (t o)", t=PACK),
                )
            else:
                nc.sync.dma_start(
                    out=rows[:].rearrange("w (g r) -> w g r", g=4),
                    in_=f_second[i, j, piece].rearrange("q (hi w t) o -> w (q hi) (t o)", hi=2, t=PACK),
                )

        def load_first_w(piece, hi):
            if (0, piece) not in w_raw:
                w_raw[(0, piece)] = raw_pool.tile([P, RAW], BF16, tag="raw", name="w_rows")
            part = w_raw[(0, piece)][:, hi * RAW // 2 : (hi + 1) * RAW // 2]
            nc.sync.dma_start(
                out=part.rearrange("w (t o) -> w t o", t=PACK),
                in_=f_first[0, 0, piece].rearrange("q (c t) (h o) -> h (q c) t o", t=PACK, h=2)[hi],
            )

        def load(half):
            load_w(half, 0)
            load_x(half, 0)
            load_w(half, 1)
            load_x(half, 1)

        def transpose_x(half, p):
            words = x_raw[half][:].bitcast(F32)
            for q2 in range(2):
                bank = psum_x.tile([P, 4, P], F32, tag="x_bank")
                x_banks[(half, p, q2)] = bank
                for a in range(4):
                    x2, u = divmod(a, 2)
                    first = (8 * p + 2 * (2 * x2 + q2)) * P
                    nc.tensor.transpose(bank[:, a, :], words[:, first + u : first + 2 * P : 2], identity[:])

        def copy_x(half, p):
            grouped = grouped_pool.tile([P, PACK * COLS], BF16, tag="x_grouped", align_bytes=64)
            x_grouped[(half, p)] = grouped
            for q2 in range(2):
                nc.scalar.copy(
                    out=grouped[:]
                    .bitcast(F32)
                    .rearrange("w (p2 q2 s a) -> w q2 p2 s a", p2=2, q2=2, a=4)[:, q2],
                    in_=x_banks[(half, p, q2)][:].rearrange("w a (s p2) -> w p2 s a", p2=2),
                )

        def quantise_x(half, p):
            if p == 0:
                codes = code_pool.tile([P, 2 * COLS], U32, tag="x_codes", align_bytes=64)
                scales = code_pool.tile([P, 2 * COLS], U8, tag="x_scales", align_bytes=64)
                x_mx[half] = (codes, scales)
            codes, scales = x_mx[half]
            cols = slice(p * COLS, (p + 1) * COLS)
            nc.vector.quantize_mx(
                out=codes[:, cols].bitcast(FP8X4), scales=scales[:, cols], in_=x_grouped[(half, p)][:]
            )

        def grouped_w(w_set, quarter):
            piece = quarter // 2
            if (w_set, piece) not in w_grouped:
                w_grouped[(w_set, piece)] = grouped_pool.tile(
                    [P, RAW], BF16, tag="w_grouped", name="w_grouped", align_bytes=64, bufs=5
                )
            return w_grouped[(w_set, piece)][:, quarter % 2 * PACK * QUARTER : (quarter % 2 + 1) * PACK * QUARTER]

        def views_w(w_set, quarter):
            grouped = grouped_w(w_set, quarter)
            rows = w_raw[(w_set, quarter // 2)]
            if w_set % 2 == 0:
                order = "w (h t g c i) -> w h g c t i" if w_set == 0 else "w (t h g c i) -> w h g c t i"
                source = rows[:].rearrange(order, t=PACK, h=2, g=2, i=4)[:, quarter % 2]
                columns = grouped.rearrange("w (i g c t) -> w g c t i", i=4, g=2, t=PACK)
            else:
                source = rows[:].rearrange("w (h g t c i) -> w h g c t i", h=2, g=2, t=PACK, i=4)[:, quarter % 2]
                columns = grouped.rearrange("w (g c i t) -> w g c t i", g=2, i=4, t=PACK)
            return columns, source

        def scalar_parts(w_set):
            return SCALAR_PARTS[w_set % 2] if w_set > 1 else FIRST_SCALAR_PARTS[w_set]

        def regroup_w_scalar(w_set, quarter):
            columns, source = views_w(w_set, quarter)
            for part in range(scalar_parts(w_set)[quarter]):
                nc.scalar.copy(out=columns[:, part], in_=source[:, part])

        def regroup_w(w_set, quarter):
            grouped = grouped_w(w_set, quarter)
            rows = w_raw[(w_set, quarter // 2)]
            mine = scalar_parts(w_set)[quarter]
            if mine == 2:
                return
            if w_set % 2 == 0:
                order = "w (h t c k i) -> w h c t k i" if w_set == 0 else "w (t h c k i) -> w h c t k i"
                source = rows[:].rearrange(order, t=PACK, h=2, k=2, i=4)[:, quarter % 2]
                columns = grouped.rearrange("w (i c k t) -> w c t k i", i=4, k=2, t=PACK)
                first = 32 * mine
                nc.vector.tensor_copy(out=columns[:, first:], in_=source[:, first:])
            else:
                source = rows[:].rearrange("w (h g t c i) -> w h g c t i", h=2, g=2, t=PACK, i=8)[:, quarter % 2]
                columns = grouped.rearrange("w (g c i t) -> w g c t i", g=2, i=8, t=PACK)
                if mine == 0:
                    nc.vector.tensor_copy(out=columns, in_=source)
                else:
                    nc.vector.tensor_copy(out=columns[:, 1], in_=source[:, 1])

        def quantise_w(w_set, quarter, count=1):
            if w_set not in w_mx:
                codes = set_pool.tile([P, SET_WORDS], U32, tag="w_codes", align_bytes=64)
                scales = set_pool.tile([P, SET_WORDS], U8, tag="w_scales", align_bytes=64)
                w_mx[w_set] = (codes, scales)
            codes, scales = w_mx[w_set]
            cols = slice(quarter * QUARTER, (quarter + count) * QUARTER)
            first = quarter % 2 * PACK * QUARTER
            nc.vector.quantize_mx(
                out=codes[:, cols].bitcast(FP8X4),
                scales=scales[:, cols],
                in_=w_grouped[(w_set, quarter // 2)][:, first : first + count * PACK * QUARTER],
            )

        def first_conv(half, chunk):
            node = half // 2
            w_codes, w_scales = w_mx[2 * node]
            x_codes, x_scales = x_mx[half]
            if (half, chunk) not in h_banks:
                h_banks[(half, chunk)] = psum_h.tile([P, COLS], F32, tag="acc_h", name="acc_h")
            acc = h_banks[(half, chunk)]
            for p in range(2):
                w_cols = slice(p * C_MID + chunk * P, p * C_MID + (chunk + 1) * P)
                x_cols = slice(p * COLS, (p + 1) * COLS)
                nc.tensor.matmul_mx(
                    out=acc[:],
                    lhsT=w_codes[:, w_cols].bitcast(FP8X4),
                    lhsT_scale=w_scales[:, w_cols],
                    rhs=x_codes[:, x_cols].bitcast(FP8X4),
                    rhs_scale=x_scales[:, x_cols],
                    start=(p == 0),
                    stop=(p == 1),
                )

        def keep_warm(half, p):
            if (half, 0) not in h_banks:
                h_banks[(half, 0)] = psum_h.tile([P, COLS], F32, tag="acc_h", name="acc_h")
            for run in range(2):
                nc.tensor.matmul(
                    out=h_banks[(half, 0)][:],
                    lhsT=identity_bf16[:],
                    rhs=x_grouped[(half, p)][:, run * COLS : (run + 1) * COLS],
                    start=True,
                    stop=True,
                )

        def warm_up():
            h_banks[(0, 0)] = psum_h.tile([P, COLS], F32, tag="acc_h", name="acc_h")
            for turn in range(WARM_UP):
                nc.tensor.matmul(out=h_banks[(0, 0)][:, :P], lhsT=ones[:], rhs=ones[:], start=True, stop=True)

        def relu_h(half, chunk):
            node = half // 2
            if (half, chunk // 4) not in h_raw:
                h_raw[(half, chunk // 4)] = grouped_pool.tile(
                    [P, 4 * COLS], BF16, tag="h_raw", name="h_raw", align_bytes=64
                )
            nc.scalar.activation(
                out=h_raw[(half, chunk // 4)][:, chunk % 4 * COLS : (chunk % 4 + 1) * COLS],
                in_=h_banks[(half, chunk)][:],
                func=RELU,
                bias=bias_first[:, chunk % 4, 2 * node + chunk // 4 : 2 * node + chunk // 4 + 1],
                scale=1.0,
            )

        def regroup_h(half, group, part=slice(0, COLS)):
            if (half, group) not in h_grouped:
                h_grouped[(half, group)] = grouped_pool.tile(
                    [P, PACK * COLS], BF16, tag="h_grouped", name="h_grouped", align_bytes=64
                )
            runs = slice(part.start // 8, part.stop // 8)
            nc.vector.tensor_copy(
                out=h_grouped[(half, group)][:].rearrange("w (c i t) -> w c t i", i=8, t=PACK)[:, runs],
                in_=h_raw[(half, group)][:].rearrange("w (t c i) -> w c t i", t=PACK, i=8)[:, runs],
            )

        def quantise_h(half, group, part=slice(0, COLS)):
            if half not in h_mx:
                codes = code_pool.tile([P, CHUNKS * P], U32, tag="h_codes", align_bytes=64)
                scales = code_pool.tile([P, CHUNKS * P], U8, tag="h_scales", align_bytes=64)
                h_mx[half] = (codes, scales)
            codes, scales = h_mx[half]
            cols = slice(group * COLS + part.start, group * COLS + part.stop)
            nc.vector.quantize_mx(
                out=codes[:, cols].bitcast(FP8X4),
                scales=scales[:, cols],
                in_=h_grouped[(half, group)][:, PACK * part.start : PACK * part.stop],
            )

        def place_biases():
            bank = psum_h.tile([P, 4, P], BF16, tag="acc_h")
            for lo in range(4):
                nc.tensor.transpose(bank[:, lo, :], rows_first[:, lo::4], identity_bf16[:])
            nc.scalar.copy(out=bias_first[:], in_=bank[:, :, 0:8])
            for part in range(2):
                cols = slice(part * COLS, (part + 1) * COLS)
                spread = psum_h.tile([P, COLS], F32, tag="acc_h")
                nc.tensor.matmul(out=spread[:], lhsT=ones[:], rhs=row_second[:, cols], start=True, stop=True)
                nc.scalar.copy(out=bias_second[:, cols], in_=spread[:])

        def second_conv(half, chunks=range(CHUNKS)):
            h_codes, h_scales = h_mx[half]
            w_codes, w_scales = w_mx[2 * (half // 2) + 1]
            if half not in acc_out:
                pool, tag = (psum_x, "x_bank") if half == HALVES - 1 else (psum_out, "acc_out")
                acc_out[half] = pool.tile([P, C_OUT], F32, tag=tag, name="acc_out")
            acc = acc_out[half]
            for chunk in chunks:
                hi, place = divmod(chunk, 4)
                h_cols = slice(chunk * P, (chunk + 1) * P)
                w_cols = slice((2 * place + hi) * C_OUT, (2 * place + hi + 1) * C_OUT)
                nc.tensor.matmul_mx(
                    out=acc[:],
                    lhsT=h_codes[:, h_cols].bitcast(FP8X4),
                    lhsT_scale=h_scales[:, h_cols],
                    rhs=w_codes[:, w_cols].bitcast(FP8X4),
                    rhs_scale=w_scales[:, w_cols],
                    start=(chunk == 0),
                    stop=(chunk == CHUNKS - 1),
                )

        def add_bias(half, cols=slice(0, C_OUT)):
            node = half // 2
            if half not in summed:
                summed[half] = out_pool.tile([P, C_OUT], F32, tag="summed", name="summed")
            nc.vector.tensor_tensor(
                out=summed[half][:, cols],
                in0=acc_out[half][:, cols],
                in1=bias_second[:, node * C_OUT + cols.start : node * C_OUT + cols.stop],
                op=ADD,
            )

        def relu_and_store(half, cols=slice(0, C_OUT)):
            i, j = divmod(half // 2, 2)
            first = (half % 2) * HALF_SAMPLES
            result = out_pool.tile([P, cols.stop - cols.start], F32, tag="result")
            nc.scalar.activation(out=result[:], in_=summed[half][:, cols], func=RELU)
            nc.sync.dma_start(
                out=out[i, j, first : first + HALF_SAMPLES].rearrange("n y x c -> (n y x) c")[:, cols], in_=result[:]
            )

        ctx.enter_context(tc.manual_schedule())
        load_first_w(0, 0)
        load_x(0, 0)
        load_first_w(1, 0)
        load_first_w(0, 1)
        load_x(0, 1)
        load_first_w(1, 1)
        for half in range(1, LOADS_AHEAD):
            load(half)
        warm_up()
        regroup_w(0, 0)
        quantise_w(0, 0)
        transpose_x(0, 0)
        copy_x(0, 0)
        place_biases()
        regroup_w(0, 2)
        quantise_x(0, 0)
        quantise_w(0, 2)
        regroup_w(0, 1)
        transpose_x(0, 1)
        copy_x(0, 1)
        keep_warm(0, 1)
        regroup_w(0, 3)
        quantise_x(0, 1)
        for chunk in range(4):
            first_conv(0, chunk)
        quantise_w(0, 1)
        quantise_w(0, 3)
        regroup_w_scalar(1, 1)
        load(LOADS_AHEAD)
        for step in range(1, HALVES):
            preparing = convolving = True
            finishing = step >= 2
            if preparing:
                transpose_x(step, 0)
            if finishing:
                quantise_h(step - 2, 1)
            if convolving:
                for chunk in range(4):
                    relu_h(step - 1, chunk)
                first_conv(step - 1, 4)
            if preparing:
                regroup_w(step, 0)
                regroup_w(step, 2)
            if finishing:
                second_conv(step - 2)
            if preparing:
                copy_x(step, 0)
            if convolving:
                regroup_h(step - 1, 0)
            if preparing:
                quantise_x(step, 0)
            if convolving:
                for chunk in (5, 6, 7):
                    first_conv(step - 1, chunk)
            if preparing:
                transpose_x(step, 1)
                keep_warm(step, 0)
            if convolving:
                relu_h(step - 1, 4)
                relu_h(step - 1, 5)
            if preparing:
                copy_x(step, 1)
            if preparing:
                keep_warm(step, 1)
            if convolving:
                quantise_h(step - 1, 0)
            if finishing:
                add_bias(step - 2)
            if convolving:
                relu_h(step - 1, 6)
                relu_h(step - 1, 7)
            if preparing:
                quantise_w(step, 0)
                regroup_w(step, 1)
                quantise_w(step, 2)
                quantise_x(step, 1)
                if step < HALVES - 1:
                    regroup_w(step, 3)
                    quantise_w(step, 1)
                for chunk in range(4):
                    first_conv(step, chunk)
            if convolving:
                regroup_h(step - 1, 1)
            if preparing:
                if step < HALVES - 1:
                    quantise_w(step, 3)
                if step + 1 < HALVES:
                    for quarter in range(4):
                        regroup_w_scalar(step + 1, quarter)
            if finishing:
                relu_and_store(step - 2)
            if preparing:
                if step + LOADS_AHEAD < HALVES:
                    load(step + LOADS_AHEAD)
        last = HALVES - 1
        left, right = slice(0, COLS // 2), slice(COLS // 2, COLS)
        quantise_h(last - 1, 1)
        first_conv(last, 4)
        relu_h(last, 1)
        relu_h(last, 0)
        first_conv(last, 5)
        first_conv(last, 6)
        relu_h(last, 3)
        relu_h(last, 2)
        first_conv(last, 7)
        for chunk in range(4, CHUNKS):
            relu_h(last, chunk)
        quantise_w(last, 1)
        regroup_w(last, 3)
        regroup_h(last, 0)
        quantise_w(last, 3)
        second_conv(last - 1)
        quantise_h(last, 0)
        second_conv(last, range(4))
        regroup_h(last, 1, left)
        regroup_h(last, 1, right)
        add_bias(last - 1)
        relu_and_store(last - 1)
        quantise_h(last, 1, left)
        second_conv(last, range(4, 6))
        quantise_h(last, 1, right)
        second_conv(last, range(6, 8))
        for cols in (slice(0, P), slice(P, C_OUT)):
            add_bias(last, cols)
            relu_and_store(last, cols)
